import numpy as np
import ml_dtypes


def mxq(x, axis, fmt="e4m3"):
    dtype, down = {"e4m3": (ml_dtypes.float8_e4m3fn, 7), "e5m2": (ml_dtypes.float8_e5m2, 14)}[fmt]
    v = np.moveaxis(np.asarray(x, np.float32).astype(ml_dtypes.bfloat16).astype(np.float64), axis, -1)
    blocks = v.reshape(v.shape[:-1] + (-1, 32))
    amax = np.abs(blocks).max(-1, keepdims=True)
    byte = np.maximum(np.where(amax > 0, np.frexp(amax)[1] - 1 + 127, 0) - down, 1)
    scale = np.exp2(byte - 127.0)
    codes = (blocks / scale).astype(np.float32).astype(dtype).astype(np.float64)
    return np.moveaxis((codes * scale).reshape(v.shape), -1, axis)


WIDE = False


def mx_kscale(k):
    if not WIDE:
        return np.ones(k)
    levels = np.array([10, -10, 5, -5, 0])
    if k % 512:
        return np.exp2(np.random.permutation(np.resize(levels, k // 32))).repeat(32)
    a = np.empty((k // 512, 16))
    for p in range(k // 512):
        a[p, :8] = np.random.permutation(np.resize(levels, 8))
        for g in range(8):
            far = levels[np.abs(levels - a[p, g]) >= 10]
            a[p, g + 8] = far[np.random.randint(len(far))]
    return np.exp2(a.ravel()).repeat(32)


BF16 = ml_dtypes.bfloat16


def bf(x):
    return np.asarray(x, np.float32).astype(BF16)


def f64(x):
    return np.asarray(x).astype(np.float64)


L, T, H, A, NH, CR, NKV, HD = 4, 1024, 1024, 512, 4, 4, 8, 128
Q = T // CR
KV = NKV * HD
RMS_EPS = 1e-5


def setup_inputs():
    s = mx_kscale(H)
    return {"cross_out": bf(np.random.standard_normal((L, Q, H)) * 3.5 / np.sqrt(T)),
            "pooled": bf(np.random.standard_normal((L, Q, H)) / np.sqrt(CR)),
            "residual_gate": bf(1.0 + 0.3 * np.random.standard_normal(1)),
            "frozen_ln": bf((1.0 + 0.1 * np.random.standard_normal((L, H))) * s),
            "frozen_k_proj": bf(np.random.standard_normal((L, KV, H)) / np.sqrt(H) / s),
            "frozen_v_proj": bf(np.random.standard_normal((L, KV, H)) / np.sqrt(H) / s)}


def reference(cross_out, pooled, residual_gate, frozen_ln, frozen_k_proj, frozen_v_proj):
    gate = 1.0 / (1.0 + np.exp(-f64(residual_gate)))
    compressed = gate * f64(cross_out) + (1.0 - gate) * f64(pooled)
    var = np.mean(compressed * compressed, axis=-1, keepdims=True)
    normed = compressed / np.sqrt(var + RMS_EPS) * f64(frozen_ln)[:, None, :]
    nq = mxq(normed, 2, "e4m3")
    k_out = nq @ mxq(f64(frozen_k_proj), 2, "e4m3").transpose(0, 2, 1)
    v_out = nq @ mxq(f64(frozen_v_proj), 2, "e4m3").transpose(0, 2, 1)
    k_out = k_out.reshape(L, Q, NKV, HD).transpose(0, 2, 1, 3)
    v_out = v_out.reshape(L, Q, NKV, HD).transpose(0, 2, 1, 3)
    return k_out, v_out

@@ -1,0 +1,254 @@
+from contextlib import ExitStack
+
+import concourse.mybir as mybir
+from concourse.masks import make_identity
+
+F32 = mybir.dt.float32
+BF16 = mybir.dt.bfloat16
+U32 = mybir.dt.uint32
+U8 = mybir.dt.uint8
+FP8X4 = mybir.dt.float8_e4m3fn_x4
+ACT = mybir.ActivationFunctionType
+ALU = mybir.AluOpType
+
+P = 128
+LAYERS = 4
+ROWS = 256
+FEATURES = 1024
+OUTPUTS = 1024
+HEAD_DIM = 128
+RMS_EPS = 1e-5
+
+ROW_TILES = ROWS // P
+PASSES = FEATURES // 512
+CHUNK = 512
+CHUNK_TILES = CHUNK // P
+CHUNK_HEADS = CHUNK // HEAD_DIM
+CHUNKS_PER_LAYER = 2 * OUTPUTS // CHUNK
+CHUNKS = LAYERS * CHUNKS_PER_LAYER
+
+LOAD_AHEAD = 4
+MULTIPLY_BEHIND = 4
+
+FLOPS = 2 * LAYERS * ROWS * FEATURES * 2 * OUTPUTS
+
+
+def tile_qformerkvcompressor_pc_kernel(
+    tc, cross_out, pooled, residual_gate, frozen_ln, frozen_k_proj, frozen_v_proj, out_0, out_1
+):
+    nc = tc.nc
+    with ExitStack() as stack:
+        stack.enter_context(tc.manual_schedule())
+        const = stack.enter_context(tc.tile_pool(name="const", bufs=1))
+        rows_in = stack.enter_context(tc.tile_pool(name="rows_in", bufs=2))
+        rows_work = stack.enter_context(tc.tile_pool(name="rows_work", bufs=1))
+        rows_mx = stack.enter_context(tc.tile_pool(name="rows_mx", bufs=2))
+        weights_in = stack.enter_context(tc.tile_pool(name="weights_in", bufs=8))
+        weights_pairs = stack.enter_context(tc.tile_pool(name="weights_pairs", bufs=3))
+        weights_mx = stack.enter_context(tc.tile_pool(name="weights_mx", bufs=5))
+        results = stack.enter_context(tc.tile_pool(name="results", bufs=5))
+        flipped = stack.enter_context(tc.psum_pool(name="flipped", bufs=5))
+        sums = stack.enter_context(tc.psum_pool(name="sums", bufs=3))
+
+        ident = const.tile([P, P], F32)
+        make_identity(nc, ident[:])
+
+        gate_logit = const.tile([P, 1], BF16)
+        nc.sync.dma_start(out=gate_logit[:], in_=residual_gate.partition_broadcast(P))
+        gate = const.tile([P, 1], F32)
+        nc.scalar.activation(out=gate[:], in_=gate_logit[:], func=ACT.Sigmoid)
+        anti_gate = const.tile([P, 1], F32)
+        nc.scalar.activation(out=anti_gate[:], in_=gate_logit[:], func=ACT.Sigmoid, scale=-1.0)
+
+        eps = const.tile([P, 1], F32)
+        nc.vector.memset(eps[:], RMS_EPS)
+        table_warm = const.tile([P, 1], F32)
+        nc.scalar.activation(out=table_warm[:], in_=eps[:], func=ACT.Sqrt)
+
+        gain_rows = const.tile([P, 4 * P], BF16)
+        nc.vector.memset(gain_rows[:], 0.0)
+        nc.sync.dma_start(
+            out=gain_rows[0 : PASSES * LAYERS, :], in_=frozen_ln.rearrange("l (g w) -> (l g) w", w=4 * P)
+        )
+        gain_bank = flipped.tile([P, 2, P], F32, tag="bank")
+        for u in range(2):
+            nc.tensor.transpose(gain_bank[:, u, :], gain_rows[:].bitcast(F32)[:, u : 2 * P : 2], ident[:])
+        gain = const.tile([P, PASSES * LAYERS, 2, 2], F32)
+        nc.vector.tensor_copy(
+            out=gain[:],
+            in_=gain_bank[:].bitcast(BF16)[:, :, 0 : 2 * PASSES * LAYERS].rearrange("p u (r e) -> p r u e", e=2),
+        )
+
+        cross_raw, pooled_raw, scaled_pooled, fused, root_mean = {}, {}, {}, {}, {}
+        rows_grouped, rows_codes, rows_scales = {}, {}, {}
+        weights_raw, pairs, weights_codes, weights_scales = {}, {}, {}, {}
+
+        def load_rows(l):
+            pooled_tile = rows_in.tile([P, ROW_TILES, FEATURES], BF16)
+            nc.sync.dma_start(out=pooled_tile[:], in_=pooled[l].rearrange("(p m) k -> p m k", m=ROW_TILES))
+            cross_tile = rows_in.tile([P, ROW_TILES, FEATURES], BF16)
+            nc.sync.dma_start(out=cross_tile[:], in_=cross_out[l].rearrange("(p m) k -> p m k", m=ROW_TILES))
+            pooled_raw[l], cross_raw[l] = pooled_tile, cross_tile
+
+        def scale_pooled(l):
+            scaled_tile = rows_work.tile([P, ROW_TILES, FEATURES], F32)
+            nc.gpsimd.tensor_scalar(
+                out=scaled_tile[:], in0=pooled_raw[l][:], scalar1=anti_gate[:, 0:1], scalar2=0.0,
+                op0=ALU.mult, op1=ALU.add,
+            )
+            scaled_pooled[l] = scaled_tile
+
+        def fuse(l):
+            fused_tile = rows_work.tile([P, ROW_TILES, FEATURES], F32)
+            nc.vector.scalar_tensor_tensor(
+                out=fused_tile[:], in0=cross_raw[l][:], scalar=gate[:, 0:1], in1=scaled_pooled[l][:],
+                op0=ALU.mult, op1=ALU.add,
+            )
+            fused[l] = fused_tile
+
+        def measure(l):
+            squares = rows_work.tile([P, ROW_TILES, FEATURES], BF16)
+            sum_squares = rows_work.tile([P, ROW_TILES], F32)
+            for m in range(ROW_TILES):
+                nc.scalar.activation(
+                    out=squares[:, m, :], in_=fused[l][:, m, :], func=ACT.Square, accum_out=sum_squares[:, m : m + 1]
+                )
+            root_tile = rows_work.tile([P, ROW_TILES], F32)
+            nc.scalar.activation(
+                out=root_tile[:], in_=sum_squares[:], func=ACT.Sqrt, bias=eps[:, 0:1], scale=1.0 / FEATURES
+            )
+            root_mean[l] = root_tile
+
+        def normalise(l):
+            inverse_root = rows_work.tile([P, ROW_TILES], F32)
+            nc.vector.reciprocal(out=inverse_root[:], in_=root_mean[l][:])
+            for m in range(ROW_TILES):
+                nc.vector.tensor_scalar(
+                    out=fused[l][:, m, :], in0=fused[l][:, m, :], scalar1=inverse_root[:, m : m + 1], scalar2=None,
+                    op0=ALU.mult,
+                )
+
+        def transpose_rows(l):
+            by_place = fused[l][:].rearrange("p m (g q u e) -> p m g u e q", g=PASSES, u=2, e=2)
+            grouped_tile = rows_work.tile([P, ROW_TILES, PASSES, P, 4], BF16, align_bytes=64)
+            for m in range(ROW_TILES):
+                for g in range(PASSES):
+                    bank = flipped.tile([P, 4, P], F32, tag="bank")
+                    for u in range(2):
+                        for e in range(2):
+                            nc.tensor.transpose(bank[:, 2 * u + e, :], by_place[:, m, g, u, e, :], ident[:])
+                    nc.vector.tensor_tensor(
+                        out=grouped_tile[:, m, g, :, :],
+                        in0=bank[:].rearrange("p t i -> p i t"),
+                        in1=gain[:, PASSES * l + g, :, :].rearrange("p u e -> p (u e)").unsqueeze(1).to_broadcast([P, P, 4]),
+                        op=ALU.mult,
+                    )
+            rows_grouped[l] = grouped_tile
+
+        def quantise_rows(l):
+            codes_tile = rows_mx.tile([P, ROW_TILES, PASSES, P], U32, align_bytes=64)
+            scales_tile = rows_mx.tile([P, ROW_TILES, PASSES, P], U8, align_bytes=64)
+            nc.vector.quantize_mx(
+                out=codes_tile[:].rearrange("p m g i -> p (m g i)").bitcast(FP8X4),
+                scales=scales_tile[:].rearrange("p m g i -> p (m g i)"),
+                in_=rows_grouped[l][:].rearrange("p m g i t -> p (m g i t)"),
+            )
+            rows_codes[l], rows_scales[l] = codes_tile, scales_tile
+
+        def place_of(j):
+            layer, rest = divmod(j, CHUNKS_PER_LAYER)
+            projection, half = divmod(rest, 2)
+            return layer, projection, half
+
+        def load_weights(j):
+            layer, projection, half = place_of(j)
+            weight = (frozen_k_proj, frozen_v_proj)[projection]
+            raw_tile = weights_in.tile([P, CHUNK_TILES, FEATURES], BF16)
+            nc.sync.dma_start(
+                out=raw_tile[:],
+                in_=weight[layer, half * CHUNK : (half + 1) * CHUNK, :].rearrange("(a p) k -> p a k", p=P),
+            )
+            weights_raw[j] = raw_tile
+
+        def transpose_weights(j):
+            words = weights_raw[j][:].bitcast(F32)
+            pairs_tile = weights_pairs.tile([P, PASSES, CHUNK, 2], F32, align_bytes=64)
+            for g in range(PASSES):
+                for side in range(2):
+                    bank = flipped.tile([P, 2, 2, P], F32, tag="bank")
+                    for u in range(2):
+                        for a in range(2):
+                            nc.tensor.transpose(
+                                bank[:, u, a, :], words[:, 2 * side + a, 2 * P * g + u : 2 * P * (g + 1) : 2], ident[:]
+                            )
+                    nc.scalar.copy(
+                        out=pairs_tile[:, g, 2 * P * side : 2 * P * (side + 1), :],
+                        in_=bank[:].rearrange("p u a o -> p (a o) u"),
+                    )
+            pairs[j] = pairs_tile
+
+        def quantise_weights(j):
+            codes_tile = weights_mx.tile([P, PASSES, CHUNK], U32, align_bytes=64)
+            scales_tile = weights_mx.tile([P, PASSES, CHUNK], U8, align_bytes=64)
+            nc.vector.quantize_mx(
+                out=codes_tile[:].rearrange("p g o -> p (g o)").bitcast(FP8X4),
+                scales=scales_tile[:].rearrange("p g o -> p (g o)"),
+                in_=pairs[j][:].rearrange("p g o u -> p (g o u)").bitcast(BF16),
+            )
+            weights_codes[j], weights_scales[j] = codes_tile, scales_tile
+
+        def multiply(j):
+            layer, projection, half = place_of(j)
+            out = (out_0, out_1)[projection]
+            result = results.tile([P, CHUNK_HEADS, ROW_TILES, HEAD_DIM], F32)
+            for m in range(ROW_TILES):
+                acc = sums.tile([P, CHUNK], F32)
+                for g in range(PASSES):
+                    nc.tensor.matmul_mx(
+                        out=acc[:],
+                        lhsT=rows_codes[layer][:, m, g, :].bitcast(FP8X4),
+                        lhsT_scale=rows_scales[layer][:, m, g, :],
+                        rhs=weights_codes[j][:, g, :].bitcast(FP8X4),
+                        rhs_scale=weights_scales[j][:, g, :],
+                        start=(g == 0),
+                        stop=(g == PASSES - 1),
+                    )
+                by_head = acc[:].rearrange("p (n d) -> p n d", d=HEAD_DIM)
+                if m == 0:
+                    nc.vector.tensor_copy(out=result[:, :, m, :], in_=by_head)
+                else:
+                    nc.scalar.copy(out=result[:, :, m, :], in_=by_head)
+            nc.sync.dma_start(
+                out=out[layer, half * CHUNK_HEADS : (half + 1) * CHUNK_HEADS].rearrange(
+                    "n (p m) d -> p n (m d)", m=ROW_TILES
+                ),
+                in_=result[:].rearrange("p n m d -> p n (m d)"),
+            )
+
+        for r in range(-2 - LOAD_AHEAD, CHUNKS + MULTIPLY_BEHIND):
+            ahead = r + LOAD_AHEAD
+            for l in range(LAYERS):
+                if ahead == CHUNKS_PER_LAYER * l - 2:
+                    load_rows(l)
+            if 0 <= ahead < CHUNKS:
+                load_weights(ahead)
+            if 0 <= r - MULTIPLY_BEHIND < CHUNKS:
+                multiply(r - MULTIPLY_BEHIND)
+            for l in range(LAYERS):
+                step = r - (CHUNKS_PER_LAYER * l - 2)
+                if step == 5:
+                    quantise_rows(l)
+                if step == 4:
+                    transpose_rows(l)
+                if step == 3:
+                    normalise(l)
+                if step == 2:
+                    measure(l)
+                if step == 1:
+                    fuse(l)
+                if step == 0:
+                    scale_pooled(l)
+            if 0 <= r < CHUNKS:
+                transpose_weights(r)
+            if 0 <= r - 1 < CHUNKS:
+                quantise_weights(r - 1)

@@ -18,6 +18,7 @@ FEATURES = 1024
 OUTPUTS = 1024
 HEAD_DIM = 128
 RMS_EPS = 1e-5
+LOGIT_BOUND = 60.0
 
 ROW_TILES = ROWS // P
 PASSES = FEATURES // 512
@@ -27,7 +28,7 @@ CHUNK_HEADS = CHUNK // HEAD_DIM
 CHUNKS_PER_LAYER = 2 * OUTPUTS // CHUNK
 CHUNKS = LAYERS * CHUNKS_PER_LAYER
 
-LOAD_AHEAD = 4
+LOAD_AHEAD = 6
 MULTIPLY_BEHIND = 4
 
 FLOPS = 2 * LAYERS * ROWS * FEATURES * 2 * OUTPUTS
@@ -43,45 +44,44 @@ def tile_qformerkvcompressor_pc_kernel(
         rows_in = stack.enter_context(tc.tile_pool(name="rows_in", bufs=2))
         rows_work = stack.enter_context(tc.tile_pool(name="rows_work", bufs=1))
         rows_mx = stack.enter_context(tc.tile_pool(name="rows_mx", bufs=2))
-        weights_in = stack.enter_context(tc.tile_pool(name="weights_in", bufs=8))
-        weights_pairs = stack.enter_context(tc.tile_pool(name="weights_pairs", bufs=3))
-        weights_mx = stack.enter_context(tc.tile_pool(name="weights_mx", bufs=5))
+        weights_in = stack.enter_context(tc.tile_pool(name="weights_in", bufs=10))
+        weights_words = stack.enter_context(tc.tile_pool(name="weights_words", bufs=3))
+        weights_mx = stack.enter_context(tc.tile_pool(name="weights_mx", bufs=6))
         results = stack.enter_context(tc.tile_pool(name="results", bufs=5))
-        flipped = stack.enter_context(tc.psum_pool(name="flipped", bufs=5))
-        sums = stack.enter_context(tc.psum_pool(name="sums", bufs=3))
+        flipped = stack.enter_context(tc.psum_pool(name="flipped", bufs=6))
+        sums = stack.enter_context(tc.psum_pool(name="sums", bufs=2))
+
+        gate_logit = const.tile([P, 1], BF16)
+        nc.scalar.dma_start(out=gate_logit[:], in_=residual_gate.partition_broadcast(P))
+        gain_rows = const.tile([P, FEATURES], BF16)
+        nc.vector.memset(gain_rows[:], 0.0)
+        nc.scalar.dma_start(out=gain_rows[0:LAYERS, :], in_=frozen_ln)
 
         ident = const.tile([P, P], F32)
         make_identity(nc, ident[:])
-
-        gate_logit = const.tile([P, 1], BF16)
-        nc.sync.dma_start(out=gate_logit[:], in_=residual_gate.partition_broadcast(P))
-        gate = const.tile([P, 1], F32)
-        nc.scalar.activation(out=gate[:], in_=gate_logit[:], func=ACT.Sigmoid)
-        anti_gate = const.tile([P, 1], F32)
-        nc.scalar.activation(out=anti_gate[:], in_=gate_logit[:], func=ACT.Sigmoid, scale=-1.0)
+        ident_bf16 = const.tile([P, P], BF16)
+        nc.vector.tensor_copy(out=ident_bf16[:], in_=ident[:])
 
         eps = const.tile([P, 1], F32)
         nc.vector.memset(eps[:], RMS_EPS)
+        clamped_logit = const.tile([P, 1], F32)
+        nc.vector.tensor_scalar(
+            out=clamped_logit[:], in0=gate_logit[:], scalar1=LOGIT_BOUND, scalar2=-LOGIT_BOUND,
+            op0=ALU.min, op1=ALU.max,
+        )
+        ratio = const.tile([P, 1], F32)
+        nc.scalar.activation(out=ratio[:], in_=clamped_logit[:], func=ACT.Exp)
+        anti_gate = const.tile([P, 1], F32)
+        nc.vector.tensor_scalar(
+            out=anti_gate[:], in0=ratio[:], scalar1=1.0, scalar2=None, op0=ALU.add
+        )
+        nc.vector.reciprocal(out=anti_gate[:], in_=anti_gate[:])
         table_warm = const.tile([P, 1], F32)
         nc.scalar.activation(out=table_warm[:], in_=eps[:], func=ACT.Sqrt)
 
-        gain_rows = const.tile([P, 4 * P], BF16)
-        nc.vector.memset(gain_rows[:], 0.0)
-        nc.sync.dma_start(
-            out=gain_rows[0 : PASSES * LAYERS, :], in_=frozen_ln.rearrange("l (g w) -> (l g) w", w=4 * P)
-        )
-        gain_bank = flipped.tile([P, 2, P], F32, tag="bank")
-        for u in range(2):
-            nc.tensor.transpose(gain_bank[:, u, :], gain_rows[:].bitcast(F32)[:, u : 2 * P : 2], ident[:])
-        gain = const.tile([P, PASSES * LAYERS, 2, 2], F32)
-        nc.vector.tensor_copy(
-            out=gain[:],
-            in_=gain_bank[:].bitcast(BF16)[:, :, 0 : 2 * PASSES * LAYERS].rearrange("p u (r e) -> p r u e", e=2),
-        )
-
-        cross_raw, pooled_raw, scaled_pooled, fused, root_mean = {}, {}, {}, {}, {}
-        rows_grouped, rows_codes, rows_scales = {}, {}, {}
-        weights_raw, pairs, weights_codes, weights_scales = {}, {}, {}, {}
+        cross_raw, pooled_raw, fused, row_scale, gain_banks, normed = {}, {}, {}, {}, {}, {}
+        rows_words, rows_codes, rows_scales = {}, {}, {}
+        weights_raw, words, weights_codes, weights_scales = {}, {}, {}, {}
 
         def load_rows(l):
             pooled_tile = rows_in.tile([P, ROW_TILES, FEATURES], BF16)
@@ -90,20 +90,13 @@ def tile_qformerkvcompressor_pc_kernel(
             nc.sync.dma_start(out=cross_tile[:], in_=cross_out[l].rearrange("(p m) k -> p m k", m=ROW_TILES))
             pooled_raw[l], cross_raw[l] = pooled_tile, cross_tile
 
-        def scale_pooled(l):
-            scaled_tile = rows_work.tile([P, ROW_TILES, FEATURES], F32)
-            nc.gpsimd.tensor_scalar(
-                out=scaled_tile[:], in0=pooled_raw[l][:], scalar1=anti_gate[:, 0:1], scalar2=0.0,
-                op0=ALU.mult, op1=ALU.add,
-            )
-            scaled_pooled[l] = scaled_tile
-
         def fuse(l):
             fused_tile = rows_work.tile([P, ROW_TILES, FEATURES], F32)
-            nc.vector.scalar_tensor_tensor(
-                out=fused_tile[:], in0=cross_raw[l][:], scalar=gate[:, 0:1], in1=scaled_pooled[l][:],
-                op0=ALU.mult, op1=ALU.add,
-            )
+            for m in range(ROW_TILES):
+                nc.vector.scalar_tensor_tensor(
+                    out=fused_tile[:, m, :], in0=cross_raw[l][:, m, :], scalar=ratio[:, 0:1],
+                    in1=pooled_raw[l][:, m, :], op0=ALU.mult, op1=ALU.add,
+                )
             fused[l] = fused_tile
 
         def measure(l):
@@ -111,39 +104,57 @@ def tile_qformerkvcompressor_pc_kernel(
             sum_squares = rows_work.tile([P, ROW_TILES], F32)
             for m in range(ROW_TILES):
                 nc.scalar.activation(
-                    out=squares[:, m, :], in_=fused[l][:, m, :], func=ACT.Square, accum_out=sum_squares[:, m : m + 1]
+                    out=squares[:, m, :], in_=fused[l][:, m, :], func=ACT.Square, scale=anti_gate[:, 0:1],
+                    accum_out=sum_squares[:, m : m + 1],
                 )
-            root_tile = rows_work.tile([P, ROW_TILES], F32)
+            root_mean = rows_work.tile([P, ROW_TILES], F32)
             nc.scalar.activation(
-                out=root_tile[:], in_=sum_squares[:], func=ACT.Sqrt, bias=eps[:, 0:1], scale=1.0 / FEATURES
+                out=root_mean[:], in_=sum_squares[:], func=ACT.Sqrt, bias=eps[:, 0:1], scale=1.0 / FEATURES
             )
-            root_mean[l] = root_tile
+            row_scale[l] = root_mean
+
+        def spread_gain(l):
+            for g in range(PASSES):
+                bank = flipped.tile([P, CHUNK], F32, tag="bank")
+                nc.tensor.matmul(
+                    bank[:], ident_bf16[:, l : l + 1].to_broadcast([P, P]), gain_rows[:, 512 * g : 512 * (g + 1)],
+                    start=True, stop=True,
+                )
+                gain_banks[l, g] = bank
 
         def normalise(l):
-            inverse_root = rows_work.tile([P, ROW_TILES], F32)
-            nc.vector.reciprocal(out=inverse_root[:], in_=root_mean[l][:])
-            for m in range(ROW_TILES):
-                nc.vector.tensor_scalar(
-                    out=fused[l][:, m, :], in0=fused[l][:, m, :], scalar1=inverse_root[:, m : m + 1], scalar2=None,
-                    op0=ALU.mult,
-                )
-
-        def transpose_rows(l):
-            by_place = fused[l][:].rearrange("p m (g q u e) -> p m g u e q", g=PASSES, u=2, e=2)
-            grouped_tile = rows_work.tile([P, ROW_TILES, PASSES, P, 4], BF16, align_bytes=64)
+            inverse = rows_work.tile([P, ROW_TILES], F32)
+            nc.vector.reciprocal(out=inverse[:], in_=row_scale[l][:])
+            scale = rows_work.tile([P, ROW_TILES], F32)
+            nc.vector.tensor_scalar(
+                out=scale[:], in0=inverse[:], scalar1=anti_gate[:, 0:1], scalar2=None, op0=ALU.mult
+            )
+            normed_tile = rows_work.tile([P, ROW_TILES, PASSES, 2, P, 2], BF16)
+            by_word = fused[l][:].rearrange("p m (g q u e) -> p m g u q e", g=PASSES, u=2, e=2)
             for m in range(ROW_TILES):
                 for g in range(PASSES):
-                    bank = flipped.tile([P, 4, P], F32, tag="bank")
                     for u in range(2):
-                        for e in range(2):
-                            nc.tensor.transpose(bank[:, 2 * u + e, :], by_place[:, m, g, u, e, :], ident[:])
-                    nc.vector.tensor_tensor(
-                        out=grouped_tile[:, m, g, :, :],
-                        in0=bank[:].rearrange("p t i -> p i t"),
-                        in1=gain[:, PASSES * l + g, :, :].rearrange("p u e -> p (u e)").unsqueeze(1).to_broadcast([P, P, 4]),
-                        op=ALU.mult,
-                    )
-            rows_grouped[l] = grouped_tile
+                        nc.vector.scalar_tensor_tensor(
+                            out=normed_tile[:, m, g, u, :, :], in0=by_word[:, m, g, u, :, :],
+                            scalar=scale[:, m : m + 1],
+                            in1=gain_banks[l, g][:].rearrange("p (q u e) -> p u q e", u=2, e=2)[:, u, :, :],
+                            op0=ALU.mult, op1=ALU.mult,
+                        )
+            normed[l] = normed_tile
+
+        def transpose_rows(l):
+            words_tile = rows_work.tile([P, ROW_TILES, PASSES, P, 2], F32, align_bytes=64)
+            for m in range(ROW_TILES):
+                bank = flipped.tile([P, PASSES, 2, P], F32, tag="bank")
+                for g in range(PASSES):
+                    for u in range(2):
+                        nc.tensor.transpose(
+                            bank[:, g, u, :],
+                            normed[l][:, m, g, u, :, :].rearrange("p q e -> p (q e)").bitcast(F32),
+                            ident[:],
+                        )
+                nc.vector.tensor_copy(out=words_tile[:, m, :, :, :], in_=bank[:].rearrange("p g u i -> p g i u"))
+            rows_words[l] = words_tile
 
         def quantise_rows(l):
             codes_tile = rows_mx.tile([P, ROW_TILES, PASSES, P], U32, align_bytes=64)
@@ -151,7 +162,7 @@ def tile_qformerkvcompressor_pc_kernel(
             nc.vector.quantize_mx(
                 out=codes_tile[:].rearrange("p m g i -> p (m g i)").bitcast(FP8X4),
                 scales=scales_tile[:].rearrange("p m g i -> p (m g i)"),
-                in_=rows_grouped[l][:].rearrange("p m g i t -> p (m g i t)"),
+                in_=rows_words[l][:].rearrange("p m g i u -> p (m g i u)").bitcast(BF16),
             )
             rows_codes[l], rows_scales[l] = codes_tile, scales_tile
 
@@ -164,28 +175,28 @@ def tile_qformerkvcompressor_pc_kernel(
             layer, projection, half = place_of(j)
             weight = (frozen_k_proj, frozen_v_proj)[projection]
             raw_tile = weights_in.tile([P, CHUNK_TILES, FEATURES], BF16)
-            nc.sync.dma_start(
-                out=raw_tile[:],
-                in_=weight[layer, half * CHUNK : (half + 1) * CHUNK, :].rearrange("(a p) k -> p a k", p=P),
-            )
+            source = weight[layer, half * CHUNK : (half + 1) * CHUNK, :].rearrange("(a p) k -> p a k", p=P)
+            if j == 0:
+                for a in range(CHUNK_TILES):
+                    nc.sync.dma_start(out=raw_tile[:, a, :], in_=source[:, a, :])
+            else:
+                nc.sync.dma_start(out=raw_tile[:], in_=source)
             weights_raw[j] = raw_tile
 
         def transpose_weights(j):
-            words = weights_raw[j][:].bitcast(F32)
-            pairs_tile = weights_pairs.tile([P, PASSES, CHUNK, 2], F32, align_bytes=64)
-            for g in range(PASSES):
-                for side in range(2):
-                    bank = flipped.tile([P, 2, 2, P], F32, tag="bank")
+            raw_words = weights_raw[j][:].bitcast(F32)
+            words_tile = weights_words.tile([P, PASSES, CHUNK, 2], F32, align_bytes=64)
+            for a in range(CHUNK_TILES):
+                bank = flipped.tile([P, PASSES, 2, P], F32, tag="bank")
+                for g in range(PASSES):
                     for u in range(2):
-                        for a in range(2):
-                            nc.tensor.transpose(
-                                bank[:, u, a, :], words[:, 2 * side + a, 2 * P * g + u : 2 * P * (g + 1) : 2], ident[:]
-                            )
-                    nc.scalar.copy(
-                        out=pairs_tile[:, g, 2 * P * side : 2 * P * (side + 1), :],
-                        in_=bank[:].rearrange("p u a o -> p (a o) u"),
-                    )
-            pairs[j] = pairs_tile
+                        nc.tensor.transpose(
+                            bank[:, g, u, :], raw_words[:, a, 2 * P * g + u : 2 * P * (g + 1) : 2], ident[:]
+                        )
+                nc.scalar.copy(
+                    out=words_tile[:, :, P * a : P * (a + 1), :], in_=bank[:].rearrange("p g u o -> p g o u")
+                )
+            words[j] = words_tile
 
         def quantise_weights(j):
             codes_tile = weights_mx.tile([P, PASSES, CHUNK], U32, align_bytes=64)
@@ -193,7 +204,7 @@ def tile_qformerkvcompressor_pc_kernel(
             nc.vector.quantize_mx(
                 out=codes_tile[:].rearrange("p g o -> p (g o)").bitcast(FP8X4),
                 scales=scales_tile[:].rearrange("p g o -> p (g o)"),
-                in_=pairs[j][:].rearrange("p g o u -> p (g o u)").bitcast(BF16),
+                in_=words[j][:].rearrange("p g o u -> p (g o u)").bitcast(BF16),
             )
             weights_codes[j], weights_scales[j] = codes_tile, scales_tile
 
@@ -225,30 +236,31 @@ def tile_qformerkvcompressor_pc_kernel(
                 in_=result[:].rearrange("p n m d -> p n (m d)"),
             )
 
-        for r in range(-2 - LOAD_AHEAD, CHUNKS + MULTIPLY_BEHIND):
+        for r in range(-1 - LOAD_AHEAD, CHUNKS + MULTIPLY_BEHIND):
             ahead = r + LOAD_AHEAD
             for l in range(LAYERS):
-                if ahead == CHUNKS_PER_LAYER * l - 2:
+                if ahead == CHUNKS_PER_LAYER * l - 1:
                     load_rows(l)
             if 0 <= ahead < CHUNKS:
                 load_weights(ahead)
             if 0 <= r - MULTIPLY_BEHIND < CHUNKS:
                 multiply(r - MULTIPLY_BEHIND)
             for l in range(LAYERS):
-                step = r - (CHUNKS_PER_LAYER * l - 2)
-                if step == 5:
-                    quantise_rows(l)
+                step = r - (CHUNKS_PER_LAYER * l - 1)
                 if step == 4:
-                    transpose_rows(l)
+                    quantise_rows(l)
                 if step == 3:
-                    normalise(l)
+                    transpose_rows(l)
                 if step == 2:
-                    measure(l)
+                    normalise(l)
                 if step == 1:
-                    fuse(l)
+                    measure(l)
                 if step == 0:
-                    scale_pooled(l)
+                    fuse(l)
             if 0 <= r < CHUNKS:
                 transpose_weights(r)
+            for l in range(LAYERS):
+                if r == CHUNKS_PER_LAYER * l:
+                    spread_gain(l)
             if 0 <= r - 1 < CHUNKS:
                 quantise_weights(r - 1)

@@ -81,7 +81,7 @@ def tile_qformerkvcompressor_pc_kernel(
 
         cross_raw, pooled_raw, fused, row_scale, gain_banks, normed = {}, {}, {}, {}, {}, {}
         rows_words, rows_codes, rows_scales = {}, {}, {}
-        weights_raw, words, weights_codes, weights_scales = {}, {}, {}, {}
+        weights_raw, words, weights_codes, weights_scales, products = {}, {}, {}, {}, {}
 
         def load_rows(l):
             pooled_tile = rows_in.tile([P, ROW_TILES, FEATURES], BF16)
@@ -183,10 +183,12 @@ def tile_qformerkvcompressor_pc_kernel(
                 nc.sync.dma_start(out=raw_tile[:], in_=source)
             weights_raw[j] = raw_tile
 
-        def transpose_weights(j):
+        def transpose_weights(j, part):
             raw_words = weights_raw[j][:].bitcast(F32)
-            words_tile = weights_words.tile([P, PASSES, CHUNK, 2], F32, align_bytes=64)
-            for a in range(CHUNK_TILES):
+            if part == 0:
+                words_tile = weights_words.tile([P, PASSES, CHUNK, 2], F32, align_bytes=64)
+                words[j] = words_tile
+            for a in range(2 * part, 2 * part + 2):
                 bank = flipped.tile([P, PASSES, 2, P], F32, tag="bank")
                 for g in range(PASSES):
                     for u in range(2):
@@ -194,9 +196,8 @@ def tile_qformerkvcompressor_pc_kernel(
                             bank[:, g, u, :], raw_words[:, a, 2 * P * g + u : 2 * P * (g + 1) : 2], ident[:]
                         )
                 nc.scalar.copy(
-                    out=words_tile[:, :, P * a : P * (a + 1), :], in_=bank[:].rearrange("p g u o -> p g o u")
+                    out=words[j][:, :, P * a : P * (a + 1), :], in_=bank[:].rearrange("p g u o -> p g o u")
                 )
-            words[j] = words_tile
 
         def quantise_weights(j):
             codes_tile = weights_mx.tile([P, PASSES, CHUNK], U32, align_bytes=64)
@@ -208,32 +209,36 @@ def tile_qformerkvcompressor_pc_kernel(
             )
             weights_codes[j], weights_scales[j] = codes_tile, scales_tile
 
-        def multiply(j):
+        def multiply(j, m):
+            layer = place_of(j)[0]
+            if m == 0:
+                result = results.tile([P, CHUNK_HEADS, ROW_TILES, HEAD_DIM], F32)
+                products[j] = result
+            acc = sums.tile([P, CHUNK], F32)
+            for g in range(PASSES):
+                nc.tensor.matmul_mx(
+                    out=acc[:],
+                    lhsT=rows_codes[layer][:, m, g, :].bitcast(FP8X4),
+                    lhsT_scale=rows_scales[layer][:, m, g, :],
+                    rhs=weights_codes[j][:, g, :].bitcast(FP8X4),
+                    rhs_scale=weights_scales[j][:, g, :],
+                    start=(g == 0),
+                    stop=(g == PASSES - 1),
+                )
+            by_head = acc[:].rearrange("p (n d) -> p n d", d=HEAD_DIM)
+            if m == 0:
+                nc.vector.tensor_copy(out=products[j][:, :, m, :], in_=by_head)
+            else:
+                nc.scalar.copy(out=products[j][:, :, m, :], in_=by_head)
+
+        def store(j):
             layer, projection, half = place_of(j)
             out = (out_0, out_1)[projection]
-            result = results.tile([P, CHUNK_HEADS, ROW_TILES, HEAD_DIM], F32)
-            for m in range(ROW_TILES):
-                acc = sums.tile([P, CHUNK], F32)
-                for g in range(PASSES):
-                    nc.tensor.matmul_mx(
-                        out=acc[:],
-                        lhsT=rows_codes[layer][:, m, g, :].bitcast(FP8X4),
-                        lhsT_scale=rows_scales[layer][:, m, g, :],
-                        rhs=weights_codes[j][:, g, :].bitcast(FP8X4),
-                        rhs_scale=weights_scales[j][:, g, :],
-                        start=(g == 0),
-                        stop=(g == PASSES - 1),
-                    )
-                by_head = acc[:].rearrange("p (n d) -> p n d", d=HEAD_DIM)
-                if m == 0:
-                    nc.vector.tensor_copy(out=result[:, :, m, :], in_=by_head)
-                else:
-                    nc.scalar.copy(out=result[:, :, m, :], in_=by_head)
             nc.sync.dma_start(
                 out=out[layer, half * CHUNK_HEADS : (half + 1) * CHUNK_HEADS].rearrange(
                     "n (p m) d -> p n (m d)", m=ROW_TILES
                 ),
-                in_=result[:].rearrange("p n m d -> p n (m d)"),
+                in_=products[j][:].rearrange("p n m d -> p n (m d)"),
             )
 
         for r in range(-1 - LOAD_AHEAD, CHUNKS + MULTIPLY_BEHIND):
@@ -244,7 +249,7 @@ def tile_qformerkvcompressor_pc_kernel(
             if 0 <= ahead < CHUNKS:
                 load_weights(ahead)
             if 0 <= r - MULTIPLY_BEHIND < CHUNKS:
-                multiply(r - MULTIPLY_BEHIND)
+                multiply(r - MULTIPLY_BEHIND, 0)
             for l in range(LAYERS):
                 step = r - (CHUNKS_PER_LAYER * l - 1)
                 if step == 4:
@@ -258,7 +263,12 @@ def tile_qformerkvcompressor_pc_kernel(
                 if step == 0:
                     fuse(l)
             if 0 <= r < CHUNKS:
-                transpose_weights(r)
+                transpose_weights(r, 0)
+            if 0 <= r - MULTIPLY_BEHIND < CHUNKS:
+                multiply(r - MULTIPLY_BEHIND, 1)
+                store(r - MULTIPLY_BEHIND)
+            if 0 <= r < CHUNKS:
+                transpose_weights(r, 1)
             for l in range(LAYERS):
                 if r == CHUNKS_PER_LAYER * l:
                     spread_gain(l)

@@ -29,7 +29,9 @@ CHUNKS_PER_LAYER = 2 * OUTPUTS // CHUNK
 CHUNKS = LAYERS * CHUNKS_PER_LAYER
 
 LOAD_AHEAD = 6
-MULTIPLY_BEHIND = 4
+MULTIPLY_BEHIND = 3
+
+SORTED = range(CHUNKS_PER_LAYER, CHUNKS)
 
 FLOPS = 2 * LAYERS * ROWS * FEATURES * 2 * OUTPUTS
 
@@ -42,28 +44,29 @@ def tile_qformerkvcompressor_pc_kernel(
         stack.enter_context(tc.manual_schedule())
         const = stack.enter_context(tc.tile_pool(name="const", bufs=1))
         rows_in = stack.enter_context(tc.tile_pool(name="rows_in", bufs=2))
-        rows_work = stack.enter_context(tc.tile_pool(name="rows_work", bufs=1))
-        rows_mx = stack.enter_context(tc.tile_pool(name="rows_mx", bufs=2))
+        rows_work = stack.enter_context(tc.tile_pool(name="rows_work", bufs=2))
+        rows_mx = stack.enter_context(tc.tile_pool(name="rows_mx", bufs=4))
         weights_in = stack.enter_context(tc.tile_pool(name="weights_in", bufs=10))
+        weights_sorted = stack.enter_context(tc.tile_pool(name="weights_sorted", bufs=2))
         weights_words = stack.enter_context(tc.tile_pool(name="weights_words", bufs=3))
         weights_mx = stack.enter_context(tc.tile_pool(name="weights_mx", bufs=6))
         results = stack.enter_context(tc.tile_pool(name="results", bufs=5))
-        flipped = stack.enter_context(tc.psum_pool(name="flipped", bufs=6))
-        sums = stack.enter_context(tc.psum_pool(name="sums", bufs=2))
+        flipped = stack.enter_context(tc.psum_pool(name="flipped", bufs=5))
+        sums = stack.enter_context(tc.psum_pool(name="sums", bufs=3))
 
         gate_logit = const.tile([P, 1], BF16)
         nc.scalar.dma_start(out=gate_logit[:], in_=residual_gate.partition_broadcast(P))
         gain_rows = const.tile([P, FEATURES], BF16)
-        nc.vector.memset(gain_rows[:], 0.0)
-        nc.scalar.dma_start(out=gain_rows[0:LAYERS, :], in_=frozen_ln)
+        nc.vector.memset(gain_rows[:].bitcast(U32), 0)
+        nc.sync.dma_start(out=gain_rows[0:LAYERS, :], in_=frozen_ln)
 
         ident = const.tile([P, P], F32)
         make_identity(nc, ident[:])
         ident_bf16 = const.tile([P, P], BF16)
         nc.vector.tensor_copy(out=ident_bf16[:], in_=ident[:])
 
-        eps = const.tile([P, 1], F32)
-        nc.vector.memset(eps[:], RMS_EPS)
+        minus_half = const.tile([P, 1], F32)
+        nc.gpsimd.memset(minus_half[:], -0.5)
         clamped_logit = const.tile([P, 1], F32)
         nc.vector.tensor_scalar(
             out=clamped_logit[:], in0=gate_logit[:], scalar1=LOGIT_BOUND, scalar2=-LOGIT_BOUND,
@@ -76,95 +79,90 @@ def tile_qformerkvcompressor_pc_kernel(
             out=anti_gate[:], in0=ratio[:], scalar1=1.0, scalar2=None, op0=ALU.add
         )
         nc.vector.reciprocal(out=anti_gate[:], in_=anti_gate[:])
-        table_warm = const.tile([P, 1], F32)
-        nc.scalar.activation(out=table_warm[:], in_=eps[:], func=ACT.Sqrt)
-
-        cross_raw, pooled_raw, fused, row_scale, gain_banks, normed = {}, {}, {}, {}, {}, {}
-        rows_words, rows_codes, rows_scales = {}, {}, {}
+        cross_raw, pooled_raw, fused, row_scale, normed, rows_words = {}, {}, {}, {}, {}, {}
+        rows_codes, rows_scales = {}, {}
+        gain = const.tile([P, LAYERS, FEATURES], BF16)
+        sorted_words = {}
         weights_raw, words, weights_codes, weights_scales, products = {}, {}, {}, {}, {}
 
         def load_rows(l):
             pooled_tile = rows_in.tile([P, ROW_TILES, FEATURES], BF16)
-            nc.sync.dma_start(out=pooled_tile[:], in_=pooled[l].rearrange("(p m) k -> p m k", m=ROW_TILES))
             cross_tile = rows_in.tile([P, ROW_TILES, FEATURES], BF16)
-            nc.sync.dma_start(out=cross_tile[:], in_=cross_out[l].rearrange("(p m) k -> p m k", m=ROW_TILES))
+            for tile, source in ((pooled_tile, pooled), (cross_tile, cross_out)):
+                nc.sync.dma_start(out=tile[:], in_=source[l].rearrange("(p m) k -> p m k", m=ROW_TILES))
             pooled_raw[l], cross_raw[l] = pooled_tile, cross_tile
 
-        def fuse(l):
-            fused_tile = rows_work.tile([P, ROW_TILES, FEATURES], F32)
-            for m in range(ROW_TILES):
-                nc.vector.scalar_tensor_tensor(
-                    out=fused_tile[:, m, :], in0=cross_raw[l][:, m, :], scalar=ratio[:, 0:1],
-                    in1=pooled_raw[l][:, m, :], op0=ALU.mult, op1=ALU.add,
-                )
-            fused[l] = fused_tile
-
-        def measure(l):
-            squares = rows_work.tile([P, ROW_TILES, FEATURES], BF16)
-            sum_squares = rows_work.tile([P, ROW_TILES], F32)
-            for m in range(ROW_TILES):
-                nc.scalar.activation(
-                    out=squares[:, m, :], in_=fused[l][:, m, :], func=ACT.Square, scale=anti_gate[:, 0:1],
-                    accum_out=sum_squares[:, m : m + 1],
-                )
-            root_mean = rows_work.tile([P, ROW_TILES], F32)
-            nc.scalar.activation(
-                out=root_mean[:], in_=sum_squares[:], func=ACT.Sqrt, bias=eps[:, 0:1], scale=1.0 / FEATURES
-            )
-            row_scale[l] = root_mean
-
         def spread_gain(l):
+            bank = flipped.tile([P, FEATURES], BF16, tag="bank")
             for g in range(PASSES):
-                bank = flipped.tile([P, CHUNK], F32, tag="bank")
                 nc.tensor.matmul(
-                    bank[:], ident_bf16[:, l : l + 1].to_broadcast([P, P]), gain_rows[:, 512 * g : 512 * (g + 1)],
-                    start=True, stop=True,
+                    bank[:, 512 * g : 512 * (g + 1)], ident_bf16[:, l : l + 1].to_broadcast([P, P]),
+                    gain_rows[:, 512 * g : 512 * (g + 1)], start=True, stop=True,
                 )
-                gain_banks[l, g] = bank
+            nc.scalar.copy(out=gain[:, l, :], in_=bank[:])
 
-        def normalise(l):
-            inverse = rows_work.tile([P, ROW_TILES], F32)
-            nc.vector.reciprocal(out=inverse[:], in_=row_scale[l][:])
-            scale = rows_work.tile([P, ROW_TILES], F32)
-            nc.vector.tensor_scalar(
-                out=scale[:], in0=inverse[:], scalar1=anti_gate[:, 0:1], scalar2=None, op0=ALU.mult
+        def fuse(l, m):
+            fused_tile = rows_work.tile([P, FEATURES], F32)
+            nc.vector.scalar_tensor_tensor(
+                out=fused_tile[:], in0=cross_raw[l][:, m, :], scalar=ratio[:, 0:1],
+                in1=pooled_raw[l][:, m, :], op0=ALU.mult, op1=ALU.add,
             )
-            normed_tile = rows_work.tile([P, ROW_TILES, PASSES, 2, P, 2], BF16)
-            by_word = fused[l][:].rearrange("p m (g q u e) -> p m g u q e", g=PASSES, u=2, e=2)
-            for m in range(ROW_TILES):
-                for g in range(PASSES):
-                    for u in range(2):
-                        nc.vector.scalar_tensor_tensor(
-                            out=normed_tile[:, m, g, u, :, :], in0=by_word[:, m, g, u, :, :],
-                            scalar=scale[:, m : m + 1],
-                            in1=gain_banks[l, g][:].rearrange("p (q u e) -> p u q e", u=2, e=2)[:, u, :, :],
-                            op0=ALU.mult, op1=ALU.mult,
-                        )
-            normed[l] = normed_tile
+            fused[l, m] = fused_tile
 
-        def transpose_rows(l):
-            words_tile = rows_work.tile([P, ROW_TILES, PASSES, P, 2], F32, align_bytes=64)
-            for m in range(ROW_TILES):
-                bank = flipped.tile([P, PASSES, 2, P], F32, tag="bank")
-                for g in range(PASSES):
-                    for u in range(2):
-                        nc.tensor.transpose(
-                            bank[:, g, u, :],
-                            normed[l][:, m, g, u, :, :].rearrange("p q e -> p (q e)").bitcast(F32),
-                            ident[:],
-                        )
-                nc.vector.tensor_copy(out=words_tile[:, m, :, :, :], in_=bank[:].rearrange("p g u i -> p g i u"))
-            rows_words[l] = words_tile
+        def measure(l, m):
+            squares = rows_work.tile([P, FEATURES], BF16)
+            sum_squares = rows_work.tile([P, 1], F32)
+            nc.scalar.activation(
+                out=squares[:], in_=fused[l, m][:], func=ACT.Square, scale=anti_gate[:, 0:1],
+                accum_out=sum_squares[:],
+            )
+            mean_square = rows_work.tile([P, 1], F32)
+            nc.gpsimd.tensor_scalar(
+                out=mean_square[:], in0=sum_squares[:], scalar1=1.0 / FEATURES, scalar2=RMS_EPS,
+                op0=ALU.mult, op1=ALU.add,
+            )
+            inverse_root = rows_work.tile([P, 1], F32)
+            nc.gpsimd.tensor_tensor(out=inverse_root[:], in0=mean_square[:], in1=minus_half[:], op=ALU.pow)
+            scale_tile = rows_work.tile([P, 1], F32)
+            nc.gpsimd.tensor_scalar(
+                out=scale_tile[:], in0=inverse_root[:], scalar1=anti_gate[:, 0:1], scalar2=0.0, op0=ALU.mult, op1=ALU.add
+            )
+            row_scale[l, m] = scale_tile
 
-        def quantise_rows(l):
-            codes_tile = rows_mx.tile([P, ROW_TILES, PASSES, P], U32, align_bytes=64)
-            scales_tile = rows_mx.tile([P, ROW_TILES, PASSES, P], U8, align_bytes=64)
+        def normalise(l, m):
+            normed_tile = rows_work.tile([P, PASSES, 2, P, 2], BF16)
+            fused_by_word = fused[l, m][:].rearrange("p (g q u e) -> p u g q e", g=PASSES, u=2, e=2)
+            gain_by_word = gain[:, l, :].rearrange("p (g q u e) -> p u g q e", g=PASSES, u=2, e=2)
+            for u in range(2):
+                nc.vector.scalar_tensor_tensor(
+                    out=normed_tile[:, :, u, :, :], in0=fused_by_word[:, u, :, :, :], scalar=row_scale[l, m][:, 0:1],
+                    in1=gain_by_word[:, u, :, :, :], op0=ALU.mult, op1=ALU.mult,
+                )
+            normed[l, m] = normed_tile
+
+        def transpose_rows(l, m):
+            words_tile = rows_work.tile([P, PASSES, P, 2], F32, align_bytes=64)
+            bank = flipped.tile([P, PASSES, 2, P], F32, tag="bank")
+            for g in range(PASSES):
+                for u in range(2):
+                    nc.tensor.transpose(
+                        bank[:, g, u, :],
+                        normed[l, m][:, g, u, :, :].rearrange("p q e -> p (q e)").bitcast(F32),
+                        ident[:],
+                    )
+            empty = nc.scalar.copy if m == 0 else nc.vector.tensor_copy
+            empty(out=words_tile[:], in_=bank[:].rearrange("p g u i -> p g i u"))
+            rows_words[l, m] = words_tile
+
+        def quantise_rows(l, m):
+            codes_tile = rows_mx.tile([P, PASSES, P], U32, align_bytes=64)
+            scales_tile = rows_mx.tile([P, PASSES, P], U8, align_bytes=64)
             nc.vector.quantize_mx(
-                out=codes_tile[:].rearrange("p m g i -> p (m g i)").bitcast(FP8X4),
-                scales=scales_tile[:].rearrange("p m g i -> p (m g i)"),
-                in_=rows_words[l][:].rearrange("p m g i u -> p (m g i u)").bitcast(BF16),
+                out=codes_tile[:].rearrange("p g i -> p (g i)").bitcast(FP8X4),
+                scales=scales_tile[:].rearrange("p g i -> p (g i)"),
+                in_=rows_words[l, m][:].rearrange("p g i u -> p (g i u)").bitcast(BF16),
             )
-            rows_codes[l], rows_scales[l] = codes_tile, scales_tile
+            rows_codes[l, m], rows_scales[l, m] = codes_tile, scales_tile
 
         def place_of(j):
             layer, rest = divmod(j, CHUNKS_PER_LAYER)
@@ -183,21 +181,29 @@ def tile_qformerkvcompressor_pc_kernel(
                 nc.sync.dma_start(out=raw_tile[:], in_=source)
             weights_raw[j] = raw_tile
 
-        def transpose_weights(j, part):
-            raw_words = weights_raw[j][:].bitcast(F32)
-            if part == 0:
+        def sort_weights(j):
+            sorted_tile = weights_sorted.tile([P, PASSES, 2, P], F32)
+            nc.vector.tensor_copy(
+                out=sorted_tile[:],
+                in_=weights_raw[j][:, 0, :].bitcast(F32).rearrange("p (g q u) -> p g u q", g=PASSES, u=2),
+            )
+            sorted_words[j] = sorted_tile
+
+        def transpose_weights(j, tiles):
+            if tiles[0] == 0:
                 words_tile = weights_words.tile([P, PASSES, CHUNK, 2], F32, align_bytes=64)
                 words[j] = words_tile
-            for a in range(2 * part, 2 * part + 2):
+            for a in tiles:
                 bank = flipped.tile([P, PASSES, 2, P], F32, tag="bank")
                 for g in range(PASSES):
                     for u in range(2):
-                        nc.tensor.transpose(
-                            bank[:, g, u, :], raw_words[:, a, 2 * P * g + u : 2 * P * (g + 1) : 2], ident[:]
-                        )
-                nc.scalar.copy(
-                    out=words[j][:, :, P * a : P * (a + 1), :], in_=bank[:].rearrange("p g u o -> p g o u")
-                )
+                        if j in SORTED and a == 0:
+                            stationary = sorted_words[j][:, g, u, :]
+                        else:
+                            stationary = weights_raw[j][:, a, :].bitcast(F32)[:, 2 * P * g + u : 2 * P * (g + 1) : 2]
+                        nc.tensor.transpose(bank[:, g, u, :], stationary, ident[:])
+                empty = nc.vector.tensor_copy if j == 0 and a < 2 else nc.scalar.copy
+                empty(out=words[j][:, :, P * a : P * (a + 1), :], in_=bank[:].rearrange("p g u o -> p g o u"))
 
         def quantise_weights(j):
             codes_tile = weights_mx.tile([P, PASSES, CHUNK], U32, align_bytes=64)
@@ -218,8 +224,8 @@ def tile_qformerkvcompressor_pc_kernel(
             for g in range(PASSES):
                 nc.tensor.matmul_mx(
                     out=acc[:],
-                    lhsT=rows_codes[layer][:, m, g, :].bitcast(FP8X4),
-                    lhsT_scale=rows_scales[layer][:, m, g, :],
+                    lhsT=rows_codes[layer, m][:, g, :].bitcast(FP8X4),
+                    lhsT_scale=rows_scales[layer, m][:, g, :],
                     rhs=weights_codes[j][:, g, :].bitcast(FP8X4),
                     rhs_scale=weights_scales[j][:, g, :],
                     start=(g == 0),
@@ -241,36 +247,44 @@ def tile_qformerkvcompressor_pc_kernel(
                 in_=products[j][:].rearrange("p n m d -> p n (m d)"),
             )
 
-        for r in range(-1 - LOAD_AHEAD, CHUNKS + MULTIPLY_BEHIND):
+        def rows_at(r, lag):
+            return [
+                (l, m) for l in range(LAYERS) for m in range(ROW_TILES) if r == CHUNKS_PER_LAYER * l - 2 + m + lag
+            ]
+
+        for r in range(-2 - LOAD_AHEAD, CHUNKS + MULTIPLY_BEHIND):
             ahead = r + LOAD_AHEAD
+            done = r - MULTIPLY_BEHIND
             for l in range(LAYERS):
-                if ahead == CHUNKS_PER_LAYER * l - 1:
+                if ahead == CHUNKS_PER_LAYER * l - 2 + (1 if l else 0):
                     load_rows(l)
             if 0 <= ahead < CHUNKS:
                 load_weights(ahead)
-            if 0 <= r - MULTIPLY_BEHIND < CHUNKS:
-                multiply(r - MULTIPLY_BEHIND, 0)
             for l in range(LAYERS):
-                step = r - (CHUNKS_PER_LAYER * l - 1)
-                if step == 4:
-                    quantise_rows(l)
-                if step == 3:
-                    transpose_rows(l)
-                if step == 2:
-                    normalise(l)
-                if step == 1:
-                    measure(l)
-                if step == 0:
-                    fuse(l)
-            if 0 <= r < CHUNKS:
-                transpose_weights(r, 0)
-            if 0 <= r - MULTIPLY_BEHIND < CHUNKS:
-                multiply(r - MULTIPLY_BEHIND, 1)
-                store(r - MULTIPLY_BEHIND)
-            if 0 <= r < CHUNKS:
-                transpose_weights(r, 1)
-            for l in range(LAYERS):
-                if r == CHUNKS_PER_LAYER * l:
+                if r == (-2, -2, 0, 1)[l]:
                     spread_gain(l)
+            if 0 <= done < CHUNKS:
+                multiply(done, 0)
+            for l, m in rows_at(r, 3):
+                transpose_rows(l, m)
+            for l, m in rows_at(r, 1):
+                measure(l, m)
+            if r == 0:
+                transpose_weights(r, (0, 1))
+            for l, m in rows_at(r, 0):
+                fuse(l, m)
+            for l, m in rows_at(r, 2):
+                normalise(l, m)
+            if r + 1 in SORTED:
+                sort_weights(r + 1)
+            if 0 < r < CHUNKS:
+                transpose_weights(r, (0, 1))
+            if 0 <= done < CHUNKS:
+                multiply(done, 1)
+                store(done)
+            if 0 <= r < CHUNKS:
+                transpose_weights(r, (2, 3))
             if 0 <= r - 1 < CHUNKS:
                 quantise_weights(r - 1)
+            for l, m in rows_at(r, 3):
+                quantise_rows(l, m)

@@ -173,7 +173,7 @@ def tile_qformerkvcompressor_pc_kernel(
             layer, projection, half = place_of(j)
             weight = (frozen_k_proj, frozen_v_proj)[projection]
             raw_tile = weights_in.tile([P, CHUNK_TILES, FEATURES], BF16)
-            source = weight[layer, half * CHUNK : (half + 1) * CHUNK, :].rearrange("(a p) k -> p a k", p=P)
+            source = weight[layer, half * CHUNK : (half + 1) * CHUNK, :].rearrange("(p a) k -> p a k", p=P)
             if j == 0:
                 for a in range(CHUNK_TILES):
                     nc.sync.dma_start(out=raw_tile[:, a, :], in_=source[:, a, :])
@@ -231,11 +231,12 @@ def tile_qformerkvcompressor_pc_kernel(
                     start=(g == 0),
                     stop=(g == PASSES - 1),
                 )
-            by_head = acc[:].rearrange("p (n d) -> p n d", d=HEAD_DIM)
+            by_head = acc[:].rearrange("p (a n q) -> p n q a", a=CHUNK_TILES, n=CHUNK_HEADS)
+            in_order = products[j][:, :, m, :].rearrange("p n (q a) -> p n q a", a=CHUNK_TILES)
             if m == 0:
-                nc.vector.tensor_copy(out=products[j][:, :, m, :], in_=by_head)
+                nc.vector.tensor_copy(out=in_order, in_=by_head)
             else:
-                nc.scalar.copy(out=products[j][:, :, m, :], in_=by_head)
+                nc.scalar.copy(out=in_order, in_=by_head)
 
         def store(j):
             layer, projection, half = place_of(j)

@@ -18,7 +18,7 @@ FEATURES = 1024
 OUTPUTS = 1024
 HEAD_DIM = 128
 RMS_EPS = 1e-5
-LOGIT_BOUND = 60.0
+LOGIT_BOUND = 30.0
 
 ROW_TILES = ROWS // P
 PASSES = FEATURES // 512
@@ -65,8 +65,6 @@ def tile_qformerkvcompressor_pc_kernel(
         ident_bf16 = const.tile([P, P], BF16)
         nc.vector.tensor_copy(out=ident_bf16[:], in_=ident[:])
 
-        minus_half = const.tile([P, 1], F32)
-        nc.gpsimd.memset(minus_half[:], -0.5)
         clamped_logit = const.tile([P, 1], F32)
         nc.vector.tensor_scalar(
             out=clamped_logit[:], in0=gate_logit[:], scalar1=LOGIT_BOUND, scalar2=-LOGIT_BOUND,
@@ -74,12 +72,24 @@ def tile_qformerkvcompressor_pc_kernel(
         )
         ratio = const.tile([P, 1], F32)
         nc.scalar.activation(out=ratio[:], in_=clamped_logit[:], func=ACT.Exp)
+        one_plus_ratio = const.tile([P, 1], F32)
+        nc.vector.tensor_scalar(out=one_plus_ratio[:], in0=ratio[:], scalar1=1.0, scalar2=None, op0=ALU.add)
         anti_gate = const.tile([P, 1], F32)
+        nc.vector.reciprocal(out=anti_gate[:], in_=one_plus_ratio[:])
+        root_scale = const.tile([P, 1], F32)
         nc.vector.tensor_scalar(
-            out=anti_gate[:], in0=ratio[:], scalar1=1.0, scalar2=None, op0=ALU.add
+            out=root_scale[:], in0=one_plus_ratio[:], scalar1=one_plus_ratio[:, 0:1], scalar2=1.0 / FEATURES,
+            op0=ALU.mult, op1=ALU.mult,
         )
-        nc.vector.reciprocal(out=anti_gate[:], in_=anti_gate[:])
-        cross_raw, pooled_raw, fused, row_scale, normed, rows_words = {}, {}, {}, {}, {}, {}
+        root_bias = const.tile([P, 1], F32)
+        nc.vector.tensor_scalar(
+            out=root_bias[:], in0=one_plus_ratio[:], scalar1=one_plus_ratio[:, 0:1], scalar2=RMS_EPS,
+            op0=ALU.mult, op1=ALU.mult,
+        )
+        table_warm = const.tile([P, 1], F32)
+        nc.scalar.activation(out=table_warm[:], in_=anti_gate[:], func=ACT.Abs_reciprocal_sqrt)
+
+        cross_raw, pooled_raw, fused, sum_of_squares, row_scale, normed, rows_words = {}, {}, {}, {}, {}, {}, {}
         rows_codes, rows_scales = {}, {}
         gain = const.tile([P, LAYERS, FEATURES], BF16)
         sorted_words = {}
@@ -116,16 +126,13 @@ def tile_qformerkvcompressor_pc_kernel(
                 out=squares[:], in_=fused[l, m][:], func=ACT.Square, scale=anti_gate[:, 0:1],
                 accum_out=sum_squares[:],
             )
-            mean_square = rows_work.tile([P, 1], F32)
-            nc.gpsimd.tensor_scalar(
-                out=mean_square[:], in0=sum_squares[:], scalar1=1.0 / FEATURES, scalar2=RMS_EPS,
-                op0=ALU.mult, op1=ALU.add,
-            )
-            inverse_root = rows_work.tile([P, 1], F32)
-            nc.gpsimd.tensor_tensor(out=inverse_root[:], in0=mean_square[:], in1=minus_half[:], op=ALU.pow)
+            sum_of_squares[l, m] = sum_squares
+
+        def take_root(l, m):
             scale_tile = rows_work.tile([P, 1], F32)
-            nc.gpsimd.tensor_scalar(
-                out=scale_tile[:], in0=inverse_root[:], scalar1=anti_gate[:, 0:1], scalar2=0.0, op0=ALU.mult, op1=ALU.add
+            nc.scalar.activation(
+                out=scale_tile[:], in_=sum_of_squares[l, m][:], func=ACT.Abs_reciprocal_sqrt,
+                scale=root_scale[:, 0:1], bias=root_bias[:, 0:1],
             )
             row_scale[l, m] = scale_tile
 
@@ -238,15 +245,11 @@ def tile_qformerkvcompressor_pc_kernel(
             else:
                 nc.scalar.copy(out=in_order, in_=by_head)
 
-        def store(j):
+        def store(j, ms):
             layer, projection, half = place_of(j)
             out = (out_0, out_1)[projection]
-            nc.sync.dma_start(
-                out=out[layer, half * CHUNK_HEADS : (half + 1) * CHUNK_HEADS].rearrange(
-                    "n (p m) d -> p n (m d)", m=ROW_TILES
-                ),
-                in_=products[j][:].rearrange("p n m d -> p n (m d)"),
-            )
+            heads = out[layer, half * CHUNK_HEADS : (half + 1) * CHUNK_HEADS].rearrange("n (p m) d -> p n m d", m=ROW_TILES)
+            nc.sync.dma_start(out=heads[:, :, ms, :], in_=products[j][:, :, ms, :])
 
         def rows_at(r, lag):
             return [
@@ -266,6 +269,8 @@ def tile_qformerkvcompressor_pc_kernel(
                     spread_gain(l)
             if 0 <= done < CHUNKS:
                 multiply(done, 0)
+                if done == CHUNKS - 1:
+                    store(done, slice(0, 1))
             for l, m in rows_at(r, 3):
                 transpose_rows(l, m)
             for l, m in rows_at(r, 1):
@@ -280,12 +285,14 @@ def tile_qformerkvcompressor_pc_kernel(
                 sort_weights(r + 1)
             if 0 < r < CHUNKS:
                 transpose_weights(r, (0, 1))
+            for l, m in rows_at(r, 1):
+                take_root(l, m)
             if 0 <= done < CHUNKS:
                 multiply(done, 1)
-                store(done)
-            if 0 <= r < CHUNKS:
-                transpose_weights(r, (2, 3))
+                store(done, slice(1, 2) if done == CHUNKS - 1 else slice(0, 2))
             if 0 <= r - 1 < CHUNKS:
                 quantise_weights(r - 1)
+            if 0 <= r < CHUNKS:
+                transpose_weights(r, (2, 3))
             for l, m in rows_at(r, 3):
                 quantise_rows(l, m)

@@ -28,10 +28,8 @@ CHUNK_HEADS = CHUNK // HEAD_DIM
 CHUNKS_PER_LAYER = 2 * OUTPUTS // CHUNK
 CHUNKS = LAYERS * CHUNKS_PER_LAYER
 
-LOAD_AHEAD = 6
+LOAD_AHEAD = 5
 MULTIPLY_BEHIND = 3
-
-SORTED = range(CHUNKS_PER_LAYER, CHUNKS)
 
 FLOPS = 2 * LAYERS * ROWS * FEATURES * 2 * OUTPUTS
 
@@ -47,7 +45,6 @@ def tile_qformerkvcompressor_pc_kernel(
         rows_work = stack.enter_context(tc.tile_pool(name="rows_work", bufs=2))
         rows_mx = stack.enter_context(tc.tile_pool(name="rows_mx", bufs=4))
         weights_in = stack.enter_context(tc.tile_pool(name="weights_in", bufs=10))
-        weights_sorted = stack.enter_context(tc.tile_pool(name="weights_sorted", bufs=2))
         weights_words = stack.enter_context(tc.tile_pool(name="weights_words", bufs=3))
         weights_mx = stack.enter_context(tc.tile_pool(name="weights_mx", bufs=6))
         results = stack.enter_context(tc.tile_pool(name="results", bufs=5))
@@ -92,14 +89,20 @@ def tile_qformerkvcompressor_pc_kernel(
         cross_raw, pooled_raw, fused, sum_of_squares, row_scale, normed, rows_words = {}, {}, {}, {}, {}, {}, {}
         rows_codes, rows_scales = {}, {}
         gain = const.tile([P, LAYERS, FEATURES], BF16)
-        sorted_words = {}
         weights_raw, words, weights_codes, weights_scales, products = {}, {}, {}, {}, {}
+
+        def rows_at(r, lag):
+            return [
+                (l, m) for l in range(LAYERS) for m in range(ROW_TILES) if r == CHUNKS_PER_LAYER * l - 2 + m + lag
+            ]
 
         def load_rows(l):
             pooled_tile = rows_in.tile([P, ROW_TILES, FEATURES], BF16)
             cross_tile = rows_in.tile([P, ROW_TILES, FEATURES], BF16)
-            for tile, source in ((pooled_tile, pooled), (cross_tile, cross_out)):
-                nc.sync.dma_start(out=tile[:], in_=source[l].rearrange("(p m) k -> p m k", m=ROW_TILES))
+            for ms in (slice(0, 1), slice(1, 2)) if l == 0 else (slice(0, 2),):
+                for tile, source in ((pooled_tile, pooled), (cross_tile, cross_out)):
+                    by_partition = source[l].rearrange("(p m) k -> p m k", m=ROW_TILES)
+                    nc.sync.dma_start(out=tile[:, ms, :], in_=by_partition[:, ms, :])
             pooled_raw[l], cross_raw[l] = pooled_tile, cross_tile
 
         def spread_gain(l):
@@ -109,7 +112,8 @@ def tile_qformerkvcompressor_pc_kernel(
                     bank[:, 512 * g : 512 * (g + 1)], ident_bf16[:, l : l + 1].to_broadcast([P, P]),
                     gain_rows[:, 512 * g : 512 * (g + 1)], start=True, stop=True,
                 )
-            nc.scalar.copy(out=gain[:, l, :], in_=bank[:])
+            empty = nc.scalar.copy if l < 2 else nc.vector.tensor_copy
+            empty(out=gain[:, l, :], in_=bank[:])
 
         def fuse(l, m):
             fused_tile = rows_work.tile([P, FEATURES], F32)
@@ -157,8 +161,7 @@ def tile_qformerkvcompressor_pc_kernel(
                         normed[l, m][:, g, u, :, :].rearrange("p q e -> p (q e)").bitcast(F32),
                         ident[:],
                     )
-            empty = nc.scalar.copy if m == 0 else nc.vector.tensor_copy
-            empty(out=words_tile[:], in_=bank[:].rearrange("p g u i -> p g i u"))
+            nc.scalar.copy(out=words_tile[:], in_=bank[:].rearrange("p g u i -> p g i u"))
             rows_words[l, m] = words_tile
 
         def quantise_rows(l, m):
@@ -181,20 +184,12 @@ def tile_qformerkvcompressor_pc_kernel(
             weight = (frozen_k_proj, frozen_v_proj)[projection]
             raw_tile = weights_in.tile([P, CHUNK_TILES, FEATURES], BF16)
             source = weight[layer, half * CHUNK : (half + 1) * CHUNK, :].rearrange("(p a) k -> p a k", p=P)
-            if j == 0:
-                for a in range(CHUNK_TILES):
-                    nc.sync.dma_start(out=raw_tile[:, a, :], in_=source[:, a, :])
+            if j < 2:
+                for a in range(0, CHUNK_TILES, 1 + j):
+                    nc.sync.dma_start(out=raw_tile[:, a : a + 1 + j, :], in_=source[:, a : a + 1 + j, :])
             else:
                 nc.sync.dma_start(out=raw_tile[:], in_=source)
             weights_raw[j] = raw_tile
-
-        def sort_weights(j):
-            sorted_tile = weights_sorted.tile([P, PASSES, 2, P], F32)
-            nc.vector.tensor_copy(
-                out=sorted_tile[:],
-                in_=weights_raw[j][:, 0, :].bitcast(F32).rearrange("p (g q u) -> p g u q", g=PASSES, u=2),
-            )
-            sorted_words[j] = sorted_tile
 
         def transpose_weights(j, tiles):
             if tiles[0] == 0:
@@ -204,12 +199,13 @@ def tile_qformerkvcompressor_pc_kernel(
                 bank = flipped.tile([P, PASSES, 2, P], F32, tag="bank")
                 for g in range(PASSES):
                     for u in range(2):
-                        if j in SORTED and a == 0:
-                            stationary = sorted_words[j][:, g, u, :]
-                        else:
-                            stationary = weights_raw[j][:, a, :].bitcast(F32)[:, 2 * P * g + u : 2 * P * (g + 1) : 2]
-                        nc.tensor.transpose(bank[:, g, u, :], stationary, ident[:])
-                empty = nc.vector.tensor_copy if j == 0 and a < 2 else nc.scalar.copy
+                        nc.tensor.transpose(
+                            bank[:, g, u, :],
+                            weights_raw[j][:, a, :].bitcast(F32)[:, 2 * P * g + u : 2 * P * (g + 1) : 2],
+                            ident[:],
+                        )
+                by_vector = (a == CHUNK_TILES - 1 and rows_at(j, 1)) or (j == 0 and a < 2)
+                empty = nc.vector.tensor_copy if by_vector else nc.scalar.copy
                 empty(out=words[j][:, :, P * a : P * (a + 1), :], in_=bank[:].rearrange("p g u o -> p g o u"))
 
         def quantise_weights(j):
@@ -251,11 +247,6 @@ def tile_qformerkvcompressor_pc_kernel(
             heads = out[layer, half * CHUNK_HEADS : (half + 1) * CHUNK_HEADS].rearrange("n (p m) d -> p n m d", m=ROW_TILES)
             nc.sync.dma_start(out=heads[:, :, ms, :], in_=products[j][:, :, ms, :])
 
-        def rows_at(r, lag):
-            return [
-                (l, m) for l in range(LAYERS) for m in range(ROW_TILES) if r == CHUNKS_PER_LAYER * l - 2 + m + lag
-            ]
-
         for r in range(-2 - LOAD_AHEAD, CHUNKS + MULTIPLY_BEHIND):
             ahead = r + LOAD_AHEAD
             done = r - MULTIPLY_BEHIND
@@ -281,8 +272,6 @@ def tile_qformerkvcompressor_pc_kernel(
                 fuse(l, m)
             for l, m in rows_at(r, 2):
                 normalise(l, m)
-            if r + 1 in SORTED:
-                sort_weights(r + 1)
             if 0 < r < CHUNKS:
                 transpose_weights(r, (0, 1))
             for l, m in rows_at(r, 1):

@@ -31,6 +31,9 @@ CHUNKS = LAYERS * CHUNKS_PER_LAYER
 LOAD_AHEAD = 5
 MULTIPLY_BEHIND = 3
 
+SORTED_CHUNKS = range(CHUNKS - 3, CHUNKS)
+SORTED_TILES = 2
+
 FLOPS = 2 * LAYERS * ROWS * FEATURES * 2 * OUTPUTS
 
 
@@ -45,6 +48,7 @@ def tile_qformerkvcompressor_pc_kernel(
         rows_work = stack.enter_context(tc.tile_pool(name="rows_work", bufs=2))
         rows_mx = stack.enter_context(tc.tile_pool(name="rows_mx", bufs=4))
         weights_in = stack.enter_context(tc.tile_pool(name="weights_in", bufs=10))
+        weights_sorted = stack.enter_context(tc.tile_pool(name="weights_sorted", bufs=2))
         weights_words = stack.enter_context(tc.tile_pool(name="weights_words", bufs=3))
         weights_mx = stack.enter_context(tc.tile_pool(name="weights_mx", bufs=6))
         results = stack.enter_context(tc.tile_pool(name="results", bufs=5))
@@ -55,7 +59,6 @@ def tile_qformerkvcompressor_pc_kernel(
         nc.scalar.dma_start(out=gate_logit[:], in_=residual_gate.partition_broadcast(P))
         gain_rows = const.tile([P, FEATURES], BF16)
         nc.vector.memset(gain_rows[:].bitcast(U32), 0)
-        nc.sync.dma_start(out=gain_rows[0:LAYERS, :], in_=frozen_ln)
 
         ident = const.tile([P, P], F32)
         make_identity(nc, ident[:])
@@ -89,6 +92,7 @@ def tile_qformerkvcompressor_pc_kernel(
         cross_raw, pooled_raw, fused, sum_of_squares, row_scale, normed, rows_words = {}, {}, {}, {}, {}, {}, {}
         rows_codes, rows_scales = {}, {}
         gain = const.tile([P, LAYERS, FEATURES], BF16)
+        sorted_words = {}
         weights_raw, words, weights_codes, weights_scales, products = {}, {}, {}, {}, {}
 
         def rows_at(r, lag):
@@ -96,14 +100,14 @@ def tile_qformerkvcompressor_pc_kernel(
                 (l, m) for l in range(LAYERS) for m in range(ROW_TILES) if r == CHUNKS_PER_LAYER * l - 2 + m + lag
             ]
 
-        def load_rows(l):
-            pooled_tile = rows_in.tile([P, ROW_TILES, FEATURES], BF16)
-            cross_tile = rows_in.tile([P, ROW_TILES, FEATURES], BF16)
-            for ms in (slice(0, 1), slice(1, 2)) if l == 0 else (slice(0, 2),):
-                for tile, source in ((pooled_tile, pooled), (cross_tile, cross_out)):
-                    by_partition = source[l].rearrange("(p m) k -> p m k", m=ROW_TILES)
-                    nc.sync.dma_start(out=tile[:, ms, :], in_=by_partition[:, ms, :])
-            pooled_raw[l], cross_raw[l] = pooled_tile, cross_tile
+        def load_rows(l, ms):
+            if ms.start == 0:
+                pooled_tile = rows_in.tile([P, ROW_TILES, FEATURES], BF16)
+                cross_tile = rows_in.tile([P, ROW_TILES, FEATURES], BF16)
+                pooled_raw[l], cross_raw[l] = pooled_tile, cross_tile
+            for tiles, source in ((pooled_raw, pooled), (cross_raw, cross_out)):
+                by_partition = source[l].rearrange("(p m) k -> p m k", m=ROW_TILES)
+                nc.sync.dma_start(out=tiles[l][:, ms, :], in_=by_partition[:, ms, :])
 
         def spread_gain(l):
             bank = flipped.tile([P, FEATURES], BF16, tag="bank")
@@ -182,14 +186,22 @@ def tile_qformerkvcompressor_pc_kernel(
         def load_weights(j):
             layer, projection, half = place_of(j)
             weight = (frozen_k_proj, frozen_v_proj)[projection]
-            raw_tile = weights_in.tile([P, CHUNK_TILES, FEATURES], BF16)
-            source = weight[layer, half * CHUNK : (half + 1) * CHUNK, :].rearrange("(p a) k -> p a k", p=P)
+            raw_tile = weights_in.tile([P, 2, 2, FEATURES], BF16)
+            source = weight[layer, half * CHUNK : (half + 1) * CHUNK, :].rearrange("(b p a) k -> p b a k", p=P, a=2)
             if j < 2:
-                for a in range(0, CHUNK_TILES, 1 + j):
-                    nc.sync.dma_start(out=raw_tile[:, a : a + 1 + j, :], in_=source[:, a : a + 1 + j, :])
+                for b in range(2):
+                    nc.sync.dma_start(out=raw_tile[:, b, :, :], in_=source[:, b, :, :])
             else:
                 nc.sync.dma_start(out=raw_tile[:], in_=source)
             weights_raw[j] = raw_tile
+
+        def sort_weights(j):
+            sorted_tile = weights_sorted.tile([P, SORTED_TILES * PASSES, 2, P], F32)
+            nc.vector.tensor_copy(
+                out=sorted_tile[:],
+                in_=weights_raw[j][:, 0, :, :].bitcast(F32).rearrange("p a (g q u) -> p (a g) u q", g=PASSES, u=2),
+            )
+            sorted_words[j] = sorted_tile
 
         def transpose_weights(j, tiles):
             if tiles[0] == 0:
@@ -199,14 +211,19 @@ def tile_qformerkvcompressor_pc_kernel(
                 bank = flipped.tile([P, PASSES, 2, P], F32, tag="bank")
                 for g in range(PASSES):
                     for u in range(2):
-                        nc.tensor.transpose(
-                            bank[:, g, u, :],
-                            weights_raw[j][:, a, :].bitcast(F32)[:, 2 * P * g + u : 2 * P * (g + 1) : 2],
-                            ident[:],
-                        )
-                by_vector = (a == CHUNK_TILES - 1 and rows_at(j, 1)) or (j == 0 and a < 2)
+                        if j in SORTED_CHUNKS and a < SORTED_TILES:
+                            stationary = sorted_words[j][:, PASSES * a + g, u, :]
+                        else:
+                            raw_words = weights_raw[j][:, a // 2, a % 2, :].bitcast(F32)
+                            stationary = raw_words[:, 2 * P * g + u : 2 * P * (g + 1) : 2]
+                        nc.tensor.transpose(bank[:, g, u, :], stationary, ident[:])
+                by_vector = (a == CHUNK_TILES - 1 and j % CHUNKS_PER_LAYER == CHUNKS_PER_LAYER - 1) or (j == 0 and a < 2)
                 empty = nc.vector.tensor_copy if by_vector else nc.scalar.copy
-                empty(out=words[j][:, :, P * a : P * (a + 1), :], in_=bank[:].rearrange("p g u o -> p g o u"))
+                by_head = words[j][:].rearrange("p g (b s a q) u -> p b a g s q u", b=2, s=2, a=2)
+                empty(
+                    out=by_head[:, a // 2, a % 2, :, :, :, :],
+                    in_=bank[:].rearrange("p g u (s q) -> p g s q u", s=2),
+                )
 
         def quantise_weights(j):
             codes_tile = weights_mx.tile([P, PASSES, CHUNK], U32, align_bytes=64)
@@ -234,8 +251,8 @@ def tile_qformerkvcompressor_pc_kernel(
                     start=(g == 0),
                     stop=(g == PASSES - 1),
                 )
-            by_head = acc[:].rearrange("p (a n q) -> p n q a", a=CHUNK_TILES, n=CHUNK_HEADS)
-            in_order = products[j][:, :, m, :].rearrange("p n (q a) -> p n q a", a=CHUNK_TILES)
+            by_head = acc[:].rearrange("p (n a q) -> p n q a", a=2, n=CHUNK_HEADS)
+            in_order = products[j][:, :, m, :].rearrange("p n (q a) -> p n q a", a=2)
             if m == 0:
                 nc.vector.tensor_copy(out=in_order, in_=by_head)
             else:
@@ -250,9 +267,13 @@ def tile_qformerkvcompressor_pc_kernel(
         for r in range(-2 - LOAD_AHEAD, CHUNKS + MULTIPLY_BEHIND):
             ahead = r + LOAD_AHEAD
             done = r - MULTIPLY_BEHIND
-            for l in range(LAYERS):
-                if ahead == CHUNKS_PER_LAYER * l - 2 + (1 if l else 0):
-                    load_rows(l)
+            if ahead == -2:
+                load_rows(0, slice(0, 1))
+                nc.sync.dma_start(out=gain_rows[0:LAYERS, :], in_=frozen_ln)
+                load_rows(0, slice(1, 2))
+            for l in range(1, LAYERS):
+                if ahead == CHUNKS_PER_LAYER * l - 1:
+                    load_rows(l, slice(0, 2))
             if 0 <= ahead < CHUNKS:
                 load_weights(ahead)
             for l in range(LAYERS):
@@ -272,6 +293,8 @@ def tile_qformerkvcompressor_pc_kernel(
                 fuse(l, m)
             for l, m in rows_at(r, 2):
                 normalise(l, m)
+            if r + 1 in SORTED_CHUNKS:
+                sort_weights(r + 1)
             if 0 < r < CHUNKS:
                 transpose_weights(r, (0, 1))
             for l, m in rows_at(r, 1):

from contextlib import ExitStack

import concourse.mybir as mybir
from concourse.masks import make_identity

F32 = mybir.dt.float32
BF16 = mybir.dt.bfloat16
U32 = mybir.dt.uint32
U8 = mybir.dt.uint8
FP8X4 = mybir.dt.float8_e4m3fn_x4
ACT = mybir.ActivationFunctionType
ALU = mybir.AluOpType

P = 128
LAYERS = 4
ROWS = 256
FEATURES = 1024
OUTPUTS = 1024
HEAD_DIM = 128
RMS_EPS = 1e-5
LOGIT_BOUND = 30.0

ROW_TILES = ROWS // P
PASSES = FEATURES // 512
CHUNK = 512
CHUNK_TILES = CHUNK // P
CHUNK_HEADS = CHUNK // HEAD_DIM
CHUNKS_PER_LAYER = 2 * OUTPUTS // CHUNK
CHUNKS = LAYERS * CHUNKS_PER_LAYER

LOAD_AHEAD = 5
MULTIPLY_BEHIND = 3

SORTED_CHUNKS = range(CHUNKS - 3, CHUNKS)
SORTED_TILES = 2

FLOPS = 2 * LAYERS * ROWS * FEATURES * 2 * OUTPUTS


def tile_qformerkvcompressor_pc_kernel(
    tc, cross_out, pooled, residual_gate, frozen_ln, frozen_k_proj, frozen_v_proj, out_0, out_1
):
    nc = tc.nc
    with ExitStack() as stack:
        stack.enter_context(tc.manual_schedule())
        const = stack.enter_context(tc.tile_pool(name="const", bufs=1))
        rows_in = stack.enter_context(tc.tile_pool(name="rows_in", bufs=2))
        rows_work = stack.enter_context(tc.tile_pool(name="rows_work", bufs=2))
        rows_mx = stack.enter_context(tc.tile_pool(name="rows_mx", bufs=4))
        weights_in = stack.enter_context(tc.tile_pool(name="weights_in", bufs=10))
        weights_sorted = stack.enter_context(tc.tile_pool(name="weights_sorted", bufs=2))
        weights_words = stack.enter_context(tc.tile_pool(name="weights_words", bufs=3))
        weights_mx = stack.enter_context(tc.tile_pool(name="weights_mx", bufs=6))
        results = stack.enter_context(tc.tile_pool(name="results", bufs=5))
        flipped = stack.enter_context(tc.psum_pool(name="flipped", bufs=5))
        sums = stack.enter_context(tc.psum_pool(name="sums", bufs=3))

        gate_logit = const.tile([P, 1], BF16)
        nc.scalar.dma_start(out=gate_logit[:], in_=residual_gate.partition_broadcast(P))
        gain_rows = const.tile([P, FEATURES], BF16)
        nc.vector.memset(gain_rows[:].bitcast(U32), 0)

        ident = const.tile([P, P], F32)
        make_identity(nc, ident[:])
        ident_bf16 = const.tile([P, P], BF16)
        nc.vector.tensor_copy(out=ident_bf16[:], in_=ident[:])

        clamped_logit = const.tile([P, 1], F32)
        nc.vector.tensor_scalar(
            out=clamped_logit[:], in0=gate_logit[:], scalar1=LOGIT_BOUND, scalar2=-LOGIT_BOUND,
            op0=ALU.min, op1=ALU.max,
        )
        ratio = const.tile([P, 1], F32)
        nc.scalar.activation(out=ratio[:], in_=clamped_logit[:], func=ACT.Exp)
        one_plus_ratio = const.tile([P, 1], F32)
        nc.vector.tensor_scalar(out=one_plus_ratio[:], in0=ratio[:], scalar1=1.0, scalar2=None, op0=ALU.add)
        anti_gate = const.tile([P, 1], F32)
        nc.vector.reciprocal(out=anti_gate[:], in_=one_plus_ratio[:])
        root_scale = const.tile([P, 1], F32)
        nc.vector.tensor_scalar(
            out=root_scale[:], in0=one_plus_ratio[:], scalar1=one_plus_ratio[:, 0:1], scalar2=1.0 / FEATURES,
            op0=ALU.mult, op1=ALU.mult,
        )
        root_bias = const.tile([P, 1], F32)
        nc.vector.tensor_scalar(
            out=root_bias[:], in0=one_plus_ratio[:], scalar1=one_plus_ratio[:, 0:1], scalar2=RMS_EPS,
            op0=ALU.mult, op1=ALU.mult,
        )
        table_warm = const.tile([P, 1], F32)
        nc.scalar.activation(out=table_warm[:], in_=anti_gate[:], func=ACT.Abs_reciprocal_sqrt)

        cross_raw, pooled_raw, fused, sum_of_squares, row_scale, normed, rows_words = {}, {}, {}, {}, {}, {}, {}
        rows_codes, rows_scales = {}, {}
        gain = const.tile([P, LAYERS, FEATURES], BF16)
        sorted_words = {}
        weights_raw, words, weights_codes, weights_scales, products = {}, {}, {}, {}, {}

        def rows_at(r, lag):
            return [
                (l, m) for l in range(LAYERS) for m in range(ROW_TILES) if r == CHUNKS_PER_LAYER * l - 2 + m + lag
            ]

        def load_rows(l, ms):
            if ms.start == 0:
                pooled_tile = rows_in.tile([P, ROW_TILES, FEATURES], BF16)
                cross_tile = rows_in.tile([P, ROW_TILES, FEATURES], BF16)
                pooled_raw[l], cross_raw[l] = pooled_tile, cross_tile
            for tiles, source in ((pooled_raw, pooled), (cross_raw, cross_out)):
                by_partition = source[l].rearrange("(p m) k -> p m k", m=ROW_TILES)
                nc.sync.dma_start(out=tiles[l][:, ms, :], in_=by_partition[:, ms, :])

        def spread_gain(l):
            bank = flipped.tile([P, FEATURES], BF16, tag="bank")
            for g in range(PASSES):
                nc.tensor.matmul(
                    bank[:, 512 * g : 512 * (g + 1)], ident_bf16[:, l : l + 1].to_broadcast([P, P]),
                    gain_rows[:, 512 * g : 512 * (g + 1)], start=True, stop=True,
                )
            empty = nc.scalar.copy if l < 2 else nc.vector.tensor_copy
            empty(out=gain[:, l, :], in_=bank[:])

        def fuse(l, m):
            fused_tile = rows_work.tile([P, FEATURES], F32)
            nc.vector.scalar_tensor_tensor(
                out=fused_tile[:], in0=cross_raw[l][:, m, :], scalar=ratio[:, 0:1],
                in1=pooled_raw[l][:, m, :], op0=ALU.mult, op1=ALU.add,
            )
            fused[l, m] = fused_tile

        def measure(l, m):
            squares = rows_work.tile([P, FEATURES], BF16)
            sum_squares = rows_work.tile([P, 1], F32)
            nc.scalar.activation(
                out=squares[:], in_=fused[l, m][:], func=ACT.Square, scale=anti_gate[:, 0:1],
                accum_out=sum_squares[:],
            )
            sum_of_squares[l, m] = sum_squares

        def take_root(l, m):
            scale_tile = rows_work.tile([P, 1], F32)
            nc.scalar.activation(
                out=scale_tile[:], in_=sum_of_squares[l, m][:], func=ACT.Abs_reciprocal_sqrt,
                scale=root_scale[:, 0:1], bias=root_bias[:, 0:1],
            )
            row_scale[l, m] = scale_tile

        def normalise(l, m):
            normed_tile = rows_work.tile([P, PASSES, 2, P, 2], BF16)
            fused_by_word = fused[l, m][:].rearrange("p (g q u e) -> p u g q e", g=PASSES, u=2, e=2)
            gain_by_word = gain[:, l, :].rearrange("p (g q u e) -> p u g q e", g=PASSES, u=2, e=2)
            for u in range(2):
                nc.vector.scalar_tensor_tensor(
                    out=normed_tile[:, :, u, :, :], in0=fused_by_word[:, u, :, :, :], scalar=row_scale[l, m][:, 0:1],
                    in1=gain_by_word[:, u, :, :, :], op0=ALU.mult, op1=ALU.mult,
                )
            normed[l, m] = normed_tile

        def transpose_rows(l, m):
            words_tile = rows_work.tile([P, PASSES, P, 2], F32, align_bytes=64)
            bank = flipped.tile([P, PASSES, 2, P], F32, tag="bank")
            for g in range(PASSES):
                for u in range(2):
                    nc.tensor.transpose(
                        bank[:, g, u, :],
                        normed[l, m][:, g, u, :, :].rearrange("p q e -> p (q e)").bitcast(F32),
                        ident[:],
                    )
            nc.scalar.copy(out=words_tile[:], in_=bank[:].rearrange("p g u i -> p g i u"))
            rows_words[l, m] = words_tile

        def quantise_rows(l, m):
            codes_tile = rows_mx.tile([P, PASSES, P], U32, align_bytes=64)
            scales_tile = rows_mx.tile([P, PASSES, P], U8, align_bytes=64)
            nc.vector.quantize_mx(
                out=codes_tile[:].rearrange("p g i -> p (g i)").bitcast(FP8X4),
                scales=scales_tile[:].rearrange("p g i -> p (g i)"),
                in_=rows_words[l, m][:].rearrange("p g i u -> p (g i u)").bitcast(BF16),
            )
            rows_codes[l, m], rows_scales[l, m] = codes_tile, scales_tile

        def place_of(j):
            layer, rest = divmod(j, CHUNKS_PER_LAYER)
            projection, half = divmod(rest, 2)
            return layer, projection, half

        def load_weights(j):
            layer, projection, half = place_of(j)
            weight = (frozen_k_proj, frozen_v_proj)[projection]
            raw_tile = weights_in.tile([P, 2, 2, FEATURES], BF16)
            source = weight[layer, half * CHUNK : (half + 1) * CHUNK, :].rearrange("(b p a) k -> p b a k", p=P, a=2)
            if j < 2:
                for b in range(2):
                    nc.sync.dma_start(out=raw_tile[:, b, :, :], in_=source[:, b, :, :])
            else:
                nc.sync.dma_start(out=raw_tile[:], in_=source)
            weights_raw[j] = raw_tile

        def sort_weights(j):
            sorted_tile = weights_sorted.tile([P, SORTED_TILES * PASSES, 2, P], F32)
            nc.vector.tensor_copy(
                out=sorted_tile[:],
                in_=weights_raw[j][:, 0, :, :].bitcast(F32).rearrange("p a (g q u) -> p (a g) u q", g=PASSES, u=2),
            )
            sorted_words[j] = sorted_tile

        def transpose_weights(j, tiles):
            if tiles[0] == 0:
                words_tile = weights_words.tile([P, PASSES, CHUNK, 2], F32, align_bytes=64)
                words[j] = words_tile
            for a in tiles:
                bank = flipped.tile([P, PASSES, 2, P], F32, tag="bank")
                for g in range(PASSES):
                    for u in range(2):
                        if j in SORTED_CHUNKS and a < SORTED_TILES:
                            stationary = sorted_words[j][:, PASSES * a + g, u, :]
                        else:
                            raw_words = weights_raw[j][:, a // 2, a % 2, :].bitcast(F32)
                            stationary = raw_words[:, 2 * P * g + u : 2 * P * (g + 1) : 2]
                        nc.tensor.transpose(bank[:, g, u, :], stationary, ident[:])
                by_vector = (a == CHUNK_TILES - 1 and j % CHUNKS_PER_LAYER == CHUNKS_PER_LAYER - 1) or (j == 0 and a < 2)
                empty = nc.vector.tensor_copy if by_vector else nc.scalar.copy
                by_head = words[j][:].rearrange("p g (b s a q) u -> p b a g s q u", b=2, s=2, a=2)
                empty(
                    out=by_head[:, a // 2, a % 2, :, :, :, :],
                    in_=bank[:].rearrange("p g u (s q) -> p g s q u", s=2),
                )

        def quantise_weights(j):
            codes_tile = weights_mx.tile([P, PASSES, CHUNK], U32, align_bytes=64)
            scales_tile = weights_mx.tile([P, PASSES, CHUNK], U8, align_bytes=64)
            nc.vector.quantize_mx(
                out=codes_tile[:].rearrange("p g o -> p (g o)").bitcast(FP8X4),
                scales=scales_tile[:].rearrange("p g o -> p (g o)"),
                in_=words[j][:].rearrange("p g o u -> p (g o u)").bitcast(BF16),
            )
            weights_codes[j], weights_scales[j] = codes_tile, scales_tile

        def multiply(j, m):
            layer = place_of(j)[0]
            if m == 0:
                result = results.tile([P, CHUNK_HEADS, ROW_TILES, HEAD_DIM], F32)
                products[j] = result
            acc = sums.tile([P, CHUNK], F32)
            for g in range(PASSES):
                nc.tensor.matmul_mx(
                    out=acc[:],
                    lhsT=rows_codes[layer, m][:, g, :].bitcast(FP8X4),
                    lhsT_scale=rows_scales[layer, m][:, g, :],
                    rhs=weights_codes[j][:, g, :].bitcast(FP8X4),
                    rhs_scale=weights_scales[j][:, g, :],
                    start=(g == 0),
                    stop=(g == PASSES - 1),
                )
            by_head = acc[:].rearrange("p (n a q) -> p n q a", a=2, n=CHUNK_HEADS)
            in_order = products[j][:, :, m, :].rearrange("p n (q a) -> p n q a", a=2)
            if m == 0:
                nc.vector.tensor_copy(out=in_order, in_=by_head)
            else:
                nc.scalar.copy(out=in_order, in_=by_head)

        def store(j, ms):
            layer, projection, half = place_of(j)
            out = (out_0, out_1)[projection]
            heads = out[layer, half * CHUNK_HEADS : (half + 1) * CHUNK_HEADS].rearrange("n (p m) d -> p n m d", m=ROW_TILES)
            nc.sync.dma_start(out=heads[:, :, ms, :], in_=products[j][:, :, ms, :])

        for r in range(-2 - LOAD_AHEAD, CHUNKS + MULTIPLY_BEHIND):
            ahead = r + LOAD_AHEAD
            done = r - MULTIPLY_BEHIND
            if ahead == -2:
                load_rows(0, slice(0, 1))
                nc.sync.dma_start(out=gain_rows[0:LAYERS, :], in_=frozen_ln)
                load_rows(0, slice(1, 2))
            for l in range(1, LAYERS):
                if ahead == CHUNKS_PER_LAYER * l - 1:
                    load_rows(l, slice(0, 2))
            if 0 <= ahead < CHUNKS:
                load_weights(ahead)
            for l in range(LAYERS):
                if r == (-2, -2, 0, 1)[l]:
                    spread_gain(l)
            if 0 <= done < CHUNKS:
                multiply(done, 0)
                if done == CHUNKS - 1:
                    store(done, slice(0, 1))
            for l, m in rows_at(r, 3):
                transpose_rows(l, m)
            for l, m in rows_at(r, 1):
                measure(l, m)
            if r == 0:
                transpose_weights(r, (0, 1))
            for l, m in rows_at(r, 0):
                fuse(l, m)
            for l, m in rows_at(r, 2):
                normalise(l, m)
            if r + 1 in SORTED_CHUNKS:
                sort_weights(r + 1)
            if 0 < r < CHUNKS:
                transpose_weights(r, (0, 1))
            for l, m in rows_at(r, 1):
                take_root(l, m)
            if 0 <= done < CHUNKS:
                multiply(done, 1)
                store(done, slice(1, 2) if done == CHUNKS - 1 else slice(0, 2))
            if 0 <= r - 1 < CHUNKS:
                quantise_weights(r - 1)
            if 0 <= r < CHUNKS:
                transpose_weights(r, (2, 3))
            for l, m in rows_at(r, 3):
                quantise_rows(l, m)
